import numpy as np
import ml_dtypes


def mxq(x, axis, fmt="e4m3"):
    dtype, down = {"e4m3": (ml_dtypes.float8_e4m3fn, 7), "e5m2": (ml_dtypes.float8_e5m2, 14)}[fmt]
    v = np.moveaxis(np.asarray(x, np.float32).astype(ml_dtypes.bfloat16).astype(np.float64), axis, -1)
    blocks = v.reshape(v.shape[:-1] + (-1, 32))
    amax = np.abs(blocks).max(-1, keepdims=True)
    byte = np.maximum(np.where(amax > 0, np.frexp(amax)[1] - 1 + 127, 0) - down, 1)
    scale = np.exp2(byte - 127.0)
    codes = (blocks / scale).astype(np.float32).astype(dtype).astype(np.float64)
    return np.moveaxis((codes * scale).reshape(v.shape), -1, axis)


WIDE = False


def mx_kscale(k):
    if not WIDE:
        return np.ones(k)
    levels = np.array([10, -10, 5, -5, 0])
    a = np.random.permutation(np.resize(levels, k // 512 * 4)).reshape(k // 512, 4)
    idx = np.arange(k)
    return np.exp2(a[idx // 512, idx % 128 // 32])


BF16 = ml_dtypes.bfloat16


def bf(x):
    return np.asarray(x, np.float32).astype(BF16)


def f64(x):
    return np.asarray(x).astype(np.float64)


B, C, HH, WW = 1, 512, 32, 32
N = HH * WW


def setup_inputs():
    s, t = mx_kscale(N), mx_kscale(C)
    z = np.random.standard_normal((B, N, N)) * 2.0
    e = np.exp(z - z.max(-1, keepdims=True))
    return {"attention": bf(e / e.sum(-1, keepdims=True) * s[None, None, :]),
            "v": bf(np.random.standard_normal((B, N, C)) * 2.0 / s[None, :, None] * t[None, None, :]),
            "x": bf(np.random.standard_normal((B, C, HH, WW))),
            "Wo": bf(np.random.standard_normal((C, C)) * 2.0 / np.sqrt(C) / t[None, :]),
            "bo": bf(np.random.standard_normal(C) * 0.2)}


def reference(attention, v, x, Wo, bo):
    h = mxq(f64(attention), 2, "e4m3") @ mxq(f64(v), 1, "e4m3")
    out = mxq(f64(Wo), 1, "e4m3") @ mxq(h, 2, "e4m3").transpose(0, 2, 1)
    out = out.reshape(B, C, HH, WW) + f64(bo)[None, :, None, None]
    return f64(x) + out

@@ -1,0 +1,251 @@
+from contextlib import ExitStack
+
+import concourse.mybir as mybir
+from concourse.masks import make_identity
+
+F32 = mybir.dt.float32
+BF16 = mybir.dt.bfloat16
+U32 = mybir.dt.uint32
+U8 = mybir.dt.uint8
+FP8X4 = mybir.dt.float8_e4m3fn_x4
+ADD = mybir.AluOpType.add
+
+P = 128
+PACK = 4
+K_PASS = P * PACK
+
+TOKENS = 1024
+CHANNELS = 512
+M_PASSES = TOKENS // K_PASS
+C_TILES = CHANNELS // P
+O_TILES = CHANNELS // P
+BLOCKS = TOKENS // P
+CHUNK_BLOCKS = 2
+CHUNK = CHUNK_BLOCKS * P
+CHUNKS = BLOCKS // CHUNK_BLOCKS
+BANK_F32 = 512
+O_TILES_PER_BANK = BANK_F32 // CHUNK
+
+V_COLUMNS_ON_VECTOR = 3 * P
+
+FLOPS = 2 * TOKENS * TOKENS * CHANNELS + 2 * CHANNELS * CHANNELS * TOKENS
+
+
+def tile_visionattention_pb_kernel(tc, attention, v, x, Wo, bo, out):
+    nc = tc.nc
+
+    attention_blocks = attention.rearrange("b (k p) m -> (b k) p m", p=P)
+    v_passes = v.rearrange("b (g u q e) c -> (b g) q u (e c)", g=M_PASSES, u=2, e=2)
+    wo_tiles = Wo.rearrange("(t p) c -> p t c", p=P)
+    bo_rows_dram = bo.rearrange("(t p) -> t p", p=P)
+    x_tiles = x.rearrange("b (t p) i j -> p (b t) (i j)", p=P)
+    y_tiles = out.rearrange("b (t p) i j -> p (b t) (i j)", p=P)
+
+    with ExitStack() as ctx:
+        keep = ctx.enter_context(tc.tile_pool(name="keep", bufs=1))
+        a_raw_pool = ctx.enter_context(tc.tile_pool(name="a_raw", bufs=BLOCKS))
+        a_pool = ctx.enter_context(tc.tile_pool(name="a", bufs=2 * CHUNK_BLOCKS))
+        h_pool = ctx.enter_context(tc.tile_pool(name="h", bufs=2))
+        y_pool = ctx.enter_context(tc.tile_pool(name="y", bufs=2 * O_TILES))
+        psum_t = ctx.enter_context(tc.psum_pool(name="psum_t", bufs=4))
+        psum_h = ctx.enter_context(tc.psum_pool(name="psum_h", bufs=2))
+        psum_p = ctx.enter_context(tc.psum_pool(name="psum_p", bufs=2))
+
+        identity_f32 = keep.tile([P, P], F32)
+        make_identity(nc, identity_f32[:])
+        identity_bf16 = keep.tile([P, P], BF16)
+        make_identity(nc, identity_bf16[:])
+
+        v_raw = keep.tile([P, M_PASSES, PACK, CHANNELS], BF16)
+        wo_raw = keep.tile([P, O_TILES, CHANNELS], BF16)
+        x_sb = keep.tile([P, O_TILES, TOKENS], BF16)
+        a_raw = {}
+
+        def load_attention_chunk(k):
+            for b in range(k * CHUNK_BLOCKS, (k + 1) * CHUNK_BLOCKS):
+                raw = a_raw_pool.tile([P, TOKENS], BF16, tag="a_raw")
+                nc.sync.dma_start(out=raw[:], in_=attention_blocks[b])
+                a_raw[b] = raw
+
+        def load_x_half(half):
+            cols = slice(half * TOKENS // 2, (half + 1) * TOKENS // 2)
+            nc.sync.dma_start(out=x_sb[:, :, cols], in_=x_tiles[:, :, cols])
+
+        for g in range(M_PASSES):
+            nc.sync.dma_start(
+                out=v_raw[:, g].rearrange("q (u e) c -> q u (e c)", e=2), in_=v_passes[g]
+            )
+        load_attention_chunk(0)
+        nc.sync.dma_start(out=wo_raw[:], in_=wo_tiles)
+        load_attention_chunk(1)
+        load_attention_chunk(2)
+        load_x_half(0)
+        load_attention_chunk(3)
+        load_x_half(1)
+
+        bo_rows = keep.tile([P, P], BF16)
+        nc.vector.memset(bo_rows[:], 0.0)
+        nc.scalar.dma_start(out=bo_rows[0:O_TILES, :], in_=bo_rows_dram)
+
+        v_grouped = keep.tile([P, M_PASSES, CHANNELS, PACK], BF16, align_bytes=64)
+        v_codes = keep.tile([P, M_PASSES, CHANNELS], U32, align_bytes=64)
+        v_scales = keep.tile([P, M_PASSES, CHANNELS], U8, align_bytes=64)
+
+        def group_v(copy, g, cols):
+            copy(
+                out=v_grouped[:, g, cols, :].rearrange("p (c i) t -> p c t i", i=4),
+                in_=v_raw[:, g, :, cols].rearrange("p t (c i) -> p c t i", i=4),
+            )
+
+        for g in range(M_PASSES):
+            group_v(nc.vector.tensor_copy, g, slice(0, V_COLUMNS_ON_VECTOR))
+            group_v(nc.scalar.copy, g, slice(V_COLUMNS_ON_VECTOR, CHANNELS))
+        for g in range(M_PASSES):
+            nc.vector.quantize_mx(
+                out=v_codes[:, g, :].bitcast(FP8X4),
+                scales=v_scales[:, g, :],
+                in_=v_grouped[:, g].rearrange("p c t -> p (c t)"),
+            )
+
+        a_grouped = {}
+        a_codes = {}
+        a_scales = {}
+        h_grouped = {}
+        h_codes = {}
+        h_scales = {}
+
+        def transpose_attention(b):
+            words = a_raw[b][:].bitcast(F32)
+            transposed = psum_t.tile([P, M_PASSES * 2, P], F32, tag="transposed")
+            for s in range(M_PASSES * 2):
+                nc.tensor.transpose(
+                    transposed[:, s, :], words[:, s * P : (s + 1) * P], identity_f32[:]
+                )
+            grouped = a_pool.tile([P, M_PASSES * P * PACK], BF16, tag="a_grouped", align_bytes=64)
+            nc.scalar.copy(
+                out=grouped[:].bitcast(F32).rearrange("p (g n u) -> p g n u", g=M_PASSES, u=2),
+                in_=transposed[:].rearrange("p (g u) n -> p g n u", u=2),
+            )
+            a_grouped[b] = grouped
+
+        def quantise_attention(b):
+            codes = a_pool.tile([P, M_PASSES * P], U32, tag="a_codes", align_bytes=64)
+            scales = a_pool.tile([P, M_PASSES * P], U8, tag="a_scales", align_bytes=64)
+            nc.vector.quantize_mx(
+                out=codes[:].bitcast(FP8X4), scales=scales[:], in_=a_grouped[b][:]
+            )
+            a_codes[b] = codes
+            a_scales[b] = scales
+
+        def attend(b):
+            h_psum = psum_h.tile([P, C_TILES, P], F32, tag="h_psum")
+            for t in range(C_TILES):
+                c_cols = slice(t * P, (t + 1) * P)
+                for g in range(M_PASSES):
+                    n_cols = slice(g * P, (g + 1) * P)
+                    nc.tensor.matmul_mx(
+                        out=h_psum[:, t, :],
+                        lhsT=v_codes[:, g, c_cols].bitcast(FP8X4),
+                        lhsT_scale=v_scales[:, g, c_cols],
+                        rhs=a_codes[b][:, n_cols].bitcast(FP8X4),
+                        rhs_scale=a_scales[b][:, n_cols],
+                        start=(g == 0),
+                        stop=(g == M_PASSES - 1),
+                    )
+            k, j = divmod(b, CHUNK_BLOCKS)
+            if j == 0:
+                h_grouped[k] = h_pool.tile(
+                    [P, CHUNK, PACK], BF16, name="h_grouped", tag="h_grouped", align_bytes=64
+                )
+                h_codes[k] = h_pool.tile(
+                    [P, CHUNK], U32, name="h_codes", tag="h_codes", align_bytes=64
+                )
+                h_scales[k] = h_pool.tile(
+                    [P, CHUNK], U8, name="h_scales", tag="h_scales", align_bytes=64
+                )
+            nc.scalar.copy(
+                out=h_grouped[k][:, j * P : (j + 1) * P, :],
+                in_=h_psum[:].rearrange("p t n -> p n t"),
+            )
+
+        def quantise_h(b):
+            k, j = divmod(b, CHUNK_BLOCKS)
+            n_cols = slice(j * P, (j + 1) * P)
+            nc.vector.quantize_mx(
+                out=h_codes[k][:, n_cols].bitcast(FP8X4),
+                scales=h_scales[k][:, n_cols],
+                in_=h_grouped[k][:, n_cols, :].rearrange("p n t -> p (n t)"),
+            )
+
+        def project(k):
+            n_cols = slice(k * CHUNK, (k + 1) * CHUNK)
+            for bank_tiles in range(0, O_TILES, O_TILES_PER_BANK):
+                p_psum = psum_p.tile([P, O_TILES_PER_BANK, CHUNK], F32, tag="p_psum")
+                for i in range(O_TILES_PER_BANK):
+                    o_tile = bank_tiles + i
+                    o_cols = slice(o_tile * P, (o_tile + 1) * P)
+                    nc.tensor.matmul_mx(
+                        out=p_psum[:, i, :],
+                        lhsT=wo_codes[:, o_cols].bitcast(FP8X4),
+                        lhsT_scale=wo_scales[:, o_cols],
+                        rhs=h_codes[k][:].bitcast(FP8X4),
+                        rhs_scale=h_scales[k][:],
+                        start=True,
+                        stop=True,
+                    )
+                for i in range(O_TILES_PER_BANK):
+                    o_tile = bank_tiles + i
+                    y_sb = y_pool.tile([P, CHUNK], F32, tag="y_sb")
+                    nc.vector.scalar_tensor_tensor(
+                        out=y_sb[:],
+                        in0=p_psum[:, i, :],
+                        scalar=bo_column[:, o_tile : o_tile + 1],
+                        in1=x_sb[:, o_tile, n_cols],
+                        op0=ADD,
+                        op1=ADD,
+                    )
+                    nc.sync.dma_start(out=y_tiles[:, o_tile, n_cols], in_=y_sb[:])
+
+        for b in range(CHUNK_BLOCKS):
+            transpose_attention(b)
+        for b in range(CHUNK_BLOCKS):
+            quantise_attention(b)
+        attend(0)
+
+        wo_grouped = keep.tile([P, O_TILES, P, PACK], BF16, align_bytes=64)
+        wo_codes = keep.tile([P, CHANNELS], U32, align_bytes=64)
+        wo_scales = keep.tile([P, CHANNELS], U8, align_bytes=64)
+        for o_tile in range(O_TILES):
+            wo_psum = psum_t.tile([P, C_TILES, P], BF16, tag="transposed")
+            for t in range(C_TILES):
+                nc.tensor.transpose(
+                    wo_psum[:, t, :], wo_raw[:, o_tile, t * P : (t + 1) * P], identity_bf16[:]
+                )
+            nc.vector.tensor_copy(
+                out=wo_grouped[:, o_tile], in_=wo_psum[:].rearrange("p t o -> p o t")
+            )
+        bo_psum = psum_t.tile([P, P], BF16, tag="transposed")
+        nc.tensor.transpose(bo_psum[:], bo_rows[:], identity_bf16[:])
+        bo_column = keep.tile([P, O_TILES], F32)
+        nc.vector.tensor_copy(out=bo_column[:], in_=bo_psum[:, 0:O_TILES])
+        nc.vector.quantize_mx(
+            out=wo_codes[:].bitcast(FP8X4),
+            scales=wo_scales[:],
+            in_=wo_grouped[:].rearrange("p k o t -> p (k o t)"),
+        )
+
+        for k in range(CHUNKS):
+            first, second = k * CHUNK_BLOCKS, k * CHUNK_BLOCKS + 1
+            following = range((k + 1) * CHUNK_BLOCKS, min((k + 2) * CHUNK_BLOCKS, BLOCKS))
+            for b in following:
+                transpose_attention(b)
+            quantise_h(first)
+            for b in following:
+                quantise_attention(b)
+            if k > 0:
+                project(k - 1)
+            attend(second)
+            quantise_h(second)
+            if k + 1 < CHUNKS:
+                attend(second + 1)
+        project(CHUNKS - 1)

@@ -42,6 +42,7 @@ def tile_visionattention_pb_kernel(tc, attention, v, x, Wo, bo, out):
     y_tiles = out.rearrange("b (t p) i j -> p (b t) (i j)", p=P)
 
     with ExitStack() as ctx:
+        ctx.enter_context(tc.manual_schedule())
         keep = ctx.enter_context(tc.tile_pool(name="keep", bufs=1))
         a_raw_pool = ctx.enter_context(tc.tile_pool(name="a_raw", bufs=BLOCKS))
         a_pool = ctx.enter_context(tc.tile_pool(name="a", bufs=2 * CHUNK_BLOCKS))

@@ -26,7 +26,7 @@ CHUNKS = BLOCKS // CHUNK_BLOCKS
 BANK_F32 = 512
 O_TILES_PER_BANK = BANK_F32 // CHUNK
 
-V_COLUMNS_ON_VECTOR = 3 * P
+V_COLUMNS_ON_VECTOR = 5 * CHANNELS // 8
 
 FLOPS = 2 * TOKENS * TOKENS * CHANNELS + 2 * CHANNELS * CHANNELS * TOKENS
 
@@ -42,10 +42,8 @@ def tile_visionattention_pb_kernel(tc, attention, v, x, Wo, bo, out):
     y_tiles = out.rearrange("b (t p) i j -> p (b t) (i j)", p=P)
 
     with ExitStack() as ctx:
-        ctx.enter_context(tc.manual_schedule())
         keep = ctx.enter_context(tc.tile_pool(name="keep", bufs=1))
-        a_raw_pool = ctx.enter_context(tc.tile_pool(name="a_raw", bufs=BLOCKS))
-        a_pool = ctx.enter_context(tc.tile_pool(name="a", bufs=2 * CHUNK_BLOCKS))
+        a_pool = ctx.enter_context(tc.tile_pool(name="a", bufs=BLOCKS))
         h_pool = ctx.enter_context(tc.tile_pool(name="h", bufs=2))
         y_pool = ctx.enter_context(tc.tile_pool(name="y", bufs=2 * O_TILES))
         psum_t = ctx.enter_context(tc.psum_pool(name="psum_t", bufs=4))
@@ -62,9 +60,9 @@ def tile_visionattention_pb_kernel(tc, attention, v, x, Wo, bo, out):
         x_sb = keep.tile([P, O_TILES, TOKENS], BF16)
         a_raw = {}
 
-        def load_attention_chunk(k):
+        def load_attention(k):
             for b in range(k * CHUNK_BLOCKS, (k + 1) * CHUNK_BLOCKS):
-                raw = a_raw_pool.tile([P, TOKENS], BF16, tag="a_raw")
+                raw = a_pool.tile([P, TOKENS], BF16, tag="a_raw")
                 nc.sync.dma_start(out=raw[:], in_=attention_blocks[b])
                 a_raw[b] = raw
 
@@ -76,12 +74,12 @@ def tile_visionattention_pb_kernel(tc, attention, v, x, Wo, bo, out):
             nc.sync.dma_start(
                 out=v_raw[:, g].rearrange("q (u e) c -> q u (e c)", e=2), in_=v_passes[g]
             )
-        load_attention_chunk(0)
+        load_attention(0)
+        load_attention(1)
         nc.sync.dma_start(out=wo_raw[:], in_=wo_tiles)
-        load_attention_chunk(1)
-        load_attention_chunk(2)
+        load_attention(2)
         load_x_half(0)
-        load_attention_chunk(3)
+        load_attention(3)
         load_x_half(1)
 
         bo_rows = keep.tile([P, P], BF16)
@@ -101,82 +99,92 @@ def tile_visionattention_pb_kernel(tc, attention, v, x, Wo, bo, out):
         for g in range(M_PASSES):
             group_v(nc.vector.tensor_copy, g, slice(0, V_COLUMNS_ON_VECTOR))
             group_v(nc.scalar.copy, g, slice(V_COLUMNS_ON_VECTOR, CHANNELS))
-        for g in range(M_PASSES):
+        for cols in (slice(0, CHANNELS // 2), slice(CHANNELS // 2, CHANNELS)):
+            for g in range(M_PASSES):
+                nc.vector.quantize_mx(
+                    out=v_codes[:, g, cols].bitcast(FP8X4),
+                    scales=v_scales[:, g, cols],
+                    in_=v_grouped[:, g, cols, :].rearrange("p c t -> p (c t)"),
+                )
+
+        wo_grouped = keep.tile([P, O_TILES, P, PACK], BF16, align_bytes=64)
+        wo_codes = keep.tile([P, CHANNELS], U32, align_bytes=64)
+        wo_scales = keep.tile([P, CHANNELS], U8, align_bytes=64)
+        bo_column = keep.tile([P, O_TILES], F32)
+
+        def prepare_wo_and_bo():
+            for o_tile in range(O_TILES):
+                wo_psum = psum_t.tile([P, C_TILES, P], BF16, tag="transposed")
+                for t in range(C_TILES):
+                    nc.tensor.transpose(
+                        wo_psum[:, t, :], wo_raw[:, o_tile, t * P : (t + 1) * P], identity_bf16[:]
+                    )
+                copy_out = nc.vector.tensor_copy if o_tile % 2 == 0 else nc.scalar.copy
+                copy_out(out=wo_grouped[:, o_tile], in_=wo_psum[:].rearrange("p t o -> p o t"))
+            bo_psum = psum_t.tile([P, P], BF16, tag="transposed")
+            nc.tensor.transpose(bo_psum[:], bo_rows[:], identity_bf16[:])
+            nc.vector.tensor_copy(out=bo_column[:], in_=bo_psum[:, 0:O_TILES])
             nc.vector.quantize_mx(
-                out=v_codes[:, g, :].bitcast(FP8X4),
-                scales=v_scales[:, g, :],
-                in_=v_grouped[:, g].rearrange("p c t -> p (c t)"),
+                out=wo_codes[:].bitcast(FP8X4),
+                scales=wo_scales[:],
+                in_=wo_grouped[:].rearrange("p k o t -> p (k o t)"),
             )
 
-        a_grouped = {}
         a_codes = {}
         a_scales = {}
-        h_grouped = {}
         h_codes = {}
         h_scales = {}
 
-        def transpose_attention(b):
-            words = a_raw[b][:].bitcast(F32)
-            transposed = psum_t.tile([P, M_PASSES * 2, P], F32, tag="transposed")
-            for s in range(M_PASSES * 2):
-                nc.tensor.transpose(
-                    transposed[:, s, :], words[:, s * P : (s + 1) * P], identity_f32[:]
-                )
-            grouped = a_pool.tile([P, M_PASSES * P * PACK], BF16, tag="a_grouped", align_bytes=64)
-            nc.scalar.copy(
-                out=grouped[:].bitcast(F32).rearrange("p (g n u) -> p g n u", g=M_PASSES, u=2),
-                in_=transposed[:].rearrange("p (g u) n -> p g n u", u=2),
-            )
-            a_grouped[b] = grouped
-
-        def quantise_attention(b):
-            codes = a_pool.tile([P, M_PASSES * P], U32, tag="a_codes", align_bytes=64)
-            scales = a_pool.tile([P, M_PASSES * P], U8, tag="a_scales", align_bytes=64)
-            nc.vector.quantize_mx(
-                out=codes[:].bitcast(FP8X4), scales=scales[:], in_=a_grouped[b][:]
-            )
-            a_codes[b] = codes
-            a_scales[b] = scales
-
-        def attend(b):
-            h_psum = psum_h.tile([P, C_TILES, P], F32, tag="h_psum")
-            for t in range(C_TILES):
-                c_cols = slice(t * P, (t + 1) * P)
-                for g in range(M_PASSES):
-                    n_cols = slice(g * P, (g + 1) * P)
-                    nc.tensor.matmul_mx(
-                        out=h_psum[:, t, :],
-                        lhsT=v_codes[:, g, c_cols].bitcast(FP8X4),
-                        lhsT_scale=v_scales[:, g, c_cols],
-                        rhs=a_codes[b][:, n_cols].bitcast(FP8X4),
-                        rhs_scale=a_scales[b][:, n_cols],
-                        start=(g == 0),
-                        stop=(g == M_PASSES - 1),
+        def prepare(k):
+            for b in range(k * CHUNK_BLOCKS, (k + 1) * CHUNK_BLOCKS):
+                words = a_raw[b][:].bitcast(F32)
+                transposed = psum_t.tile([P, M_PASSES * 2, P], F32, tag="transposed")
+                for s in range(M_PASSES * 2):
+                    nc.tensor.transpose(
+                        transposed[:, s, :], words[:, s * P : (s + 1) * P], identity_f32[:]
                     )
-            k, j = divmod(b, CHUNK_BLOCKS)
-            if j == 0:
-                h_grouped[k] = h_pool.tile(
-                    [P, CHUNK, PACK], BF16, name="h_grouped", tag="h_grouped", align_bytes=64
+                grouped = a_pool.tile(
+                    [P, M_PASSES * P * PACK], BF16, tag="a_grouped", align_bytes=64
                 )
-                h_codes[k] = h_pool.tile(
-                    [P, CHUNK], U32, name="h_codes", tag="h_codes", align_bytes=64
+                nc.scalar.copy(
+                    out=grouped[:].bitcast(F32).rearrange("p (g n u) -> p g n u", g=M_PASSES, u=2),
+                    in_=transposed[:].rearrange("p (g u) n -> p g n u", u=2),
                 )
-                h_scales[k] = h_pool.tile(
-                    [P, CHUNK], U8, name="h_scales", tag="h_scales", align_bytes=64
-                )
-            nc.scalar.copy(
-                out=h_grouped[k][:, j * P : (j + 1) * P, :],
-                in_=h_psum[:].rearrange("p t n -> p n t"),
-            )
+                codes = a_pool.tile([P, M_PASSES * P], U32, tag="a_codes", align_bytes=64)
+                scales = a_pool.tile([P, M_PASSES * P], U8, tag="a_scales", align_bytes=64)
+                nc.vector.quantize_mx(out=codes[:].bitcast(FP8X4), scales=scales[:], in_=grouped[:])
+                a_codes[b] = codes
+                a_scales[b] = scales
 
-        def quantise_h(b):
-            k, j = divmod(b, CHUNK_BLOCKS)
-            n_cols = slice(j * P, (j + 1) * P)
-            nc.vector.quantize_mx(
-                out=h_codes[k][:, n_cols].bitcast(FP8X4),
-                scales=h_scales[k][:, n_cols],
-                in_=h_grouped[k][:, n_cols, :].rearrange("p n t -> p (n t)"),
-            )
+        def attend(k):
+            grouped = h_pool.tile([P, CHUNK, PACK], BF16, tag="h_grouped", align_bytes=64)
+            codes = h_pool.tile([P, CHUNK], U32, tag="h_codes", align_bytes=64)
+            scales = h_pool.tile([P, CHUNK], U8, tag="h_scales", align_bytes=64)
+            for j in range(CHUNK_BLOCKS):
+                b = k * CHUNK_BLOCKS + j
+                h_psum = psum_h.tile([P, C_TILES, P], F32, tag="h_psum")
+                for t in range(C_TILES):
+                    c_cols = slice(t * P, (t + 1) * P)
+                    for g in range(M_PASSES):
+                        g_cols = slice(g * P, (g + 1) * P)
+                        nc.tensor.matmul_mx(
+                            out=h_psum[:, t, :],
+                            lhsT=v_codes[:, g, c_cols].bitcast(FP8X4),
+                            lhsT_scale=v_scales[:, g, c_cols],
+                            rhs=a_codes[b][:, g_cols].bitcast(FP8X4),
+                            rhs_scale=a_scales[b][:, g_cols],
+                            start=(g == 0),
+                            stop=(g == M_PASSES - 1),
+                        )
+                n_cols = slice(j * P, (j + 1) * P)
+                nc.scalar.copy(out=grouped[:, n_cols, :], in_=h_psum[:].rearrange("p t n -> p n t"))
+                nc.vector.quantize_mx(
+                    out=codes[:, n_cols].bitcast(FP8X4),
+                    scales=scales[:, n_cols],
+                    in_=grouped[:, n_cols, :].rearrange("p n t -> p (n t)"),
+                )
+            h_codes[k] = codes
+            h_scales[k] = scales
 
         def project(k):
             n_cols = slice(k * CHUNK, (k + 1) * CHUNK)
@@ -207,46 +215,13 @@ def tile_visionattention_pb_kernel(tc, attention, v, x, Wo, bo, out):
                     )
                     nc.sync.dma_start(out=y_tiles[:, o_tile, n_cols], in_=y_sb[:])
 
-        for b in range(CHUNK_BLOCKS):
-            transpose_attention(b)
-        for b in range(CHUNK_BLOCKS):
-            quantise_attention(b)
+        prepare(0)
+        prepare(1)
         attend(0)
-
-        wo_grouped = keep.tile([P, O_TILES, P, PACK], BF16, align_bytes=64)
-        wo_codes = keep.tile([P, CHANNELS], U32, align_bytes=64)
-        wo_scales = keep.tile([P, CHANNELS], U8, align_bytes=64)
-        for o_tile in range(O_TILES):
-            wo_psum = psum_t.tile([P, C_TILES, P], BF16, tag="transposed")
-            for t in range(C_TILES):
-                nc.tensor.transpose(
-                    wo_psum[:, t, :], wo_raw[:, o_tile, t * P : (t + 1) * P], identity_bf16[:]
-                )
-            nc.vector.tensor_copy(
-                out=wo_grouped[:, o_tile], in_=wo_psum[:].rearrange("p t o -> p o t")
-            )
-        bo_psum = psum_t.tile([P, P], BF16, tag="transposed")
-        nc.tensor.transpose(bo_psum[:], bo_rows[:], identity_bf16[:])
-        bo_column = keep.tile([P, O_TILES], F32)
-        nc.vector.tensor_copy(out=bo_column[:], in_=bo_psum[:, 0:O_TILES])
-        nc.vector.quantize_mx(
-            out=wo_codes[:].bitcast(FP8X4),
-            scales=wo_scales[:],
-            in_=wo_grouped[:].rearrange("p k o t -> p (k o t)"),
-        )
-
+        prepare_wo_and_bo()
         for k in range(CHUNKS):
-            first, second = k * CHUNK_BLOCKS, k * CHUNK_BLOCKS + 1
-            following = range((k + 1) * CHUNK_BLOCKS, min((k + 2) * CHUNK_BLOCKS, BLOCKS))
-            for b in following:
-                transpose_attention(b)
-            quantise_h(first)
-            for b in following:
-                quantise_attention(b)
-            if k > 0:
-                project(k - 1)
-            attend(second)
-            quantise_h(second)
+            if k + 2 < CHUNKS:
+                prepare(k + 2)
+            project(k)
             if k + 1 < CHUNKS:
-                attend(second + 1)
-        project(CHUNKS - 1)
+                attend(k + 1)

from contextlib import ExitStack

import concourse.mybir as mybir
from concourse.masks import make_identity

F32 = mybir.dt.float32
BF16 = mybir.dt.bfloat16
U32 = mybir.dt.uint32
U8 = mybir.dt.uint8
FP8X4 = mybir.dt.float8_e4m3fn_x4
ADD = mybir.AluOpType.add

P = 128
PACK = 4
K_PASS = P * PACK

TOKENS = 1024
CHANNELS = 512
M_PASSES = TOKENS // K_PASS
C_TILES = CHANNELS // P
O_TILES = CHANNELS // P
BLOCKS = TOKENS // P
CHUNK_BLOCKS = 2
CHUNK = CHUNK_BLOCKS * P
CHUNKS = BLOCKS // CHUNK_BLOCKS
BANK_F32 = 512
O_TILES_PER_BANK = BANK_F32 // CHUNK

V_COLUMNS_ON_VECTOR = 5 * CHANNELS // 8

FLOPS = 2 * TOKENS * TOKENS * CHANNELS + 2 * CHANNELS * CHANNELS * TOKENS


def tile_visionattention_pb_kernel(tc, attention, v, x, Wo, bo, out):
    nc = tc.nc

    attention_blocks = attention.rearrange("b (k p) m -> (b k) p m", p=P)
    v_passes = v.rearrange("b (g u q e) c -> (b g) q u (e c)", g=M_PASSES, u=2, e=2)
    wo_tiles = Wo.rearrange("(t p) c -> p t c", p=P)
    bo_rows_dram = bo.rearrange("(t p) -> t p", p=P)
    x_tiles = x.rearrange("b (t p) i j -> p (b t) (i j)", p=P)
    y_tiles = out.rearrange("b (t p) i j -> p (b t) (i j)", p=P)

    with ExitStack() as ctx:
        keep = ctx.enter_context(tc.tile_pool(name="keep", bufs=1))
        a_pool = ctx.enter_context(tc.tile_pool(name="a", bufs=BLOCKS))
        h_pool = ctx.enter_context(tc.tile_pool(name="h", bufs=2))
        y_pool = ctx.enter_context(tc.tile_pool(name="y", bufs=2 * O_TILES))
        psum_t = ctx.enter_context(tc.psum_pool(name="psum_t", bufs=4))
        psum_h = ctx.enter_context(tc.psum_pool(name="psum_h", bufs=2))
        psum_p = ctx.enter_context(tc.psum_pool(name="psum_p", bufs=2))

        identity_f32 = keep.tile([P, P], F32)
        make_identity(nc, identity_f32[:])
        identity_bf16 = keep.tile([P, P], BF16)
        make_identity(nc, identity_bf16[:])

        v_raw = keep.tile([P, M_PASSES, PACK, CHANNELS], BF16)
        wo_raw = keep.tile([P, O_TILES, CHANNELS], BF16)
        x_sb = keep.tile([P, O_TILES, TOKENS], BF16)
        a_raw = {}

        def load_attention(k):
            for b in range(k * CHUNK_BLOCKS, (k + 1) * CHUNK_BLOCKS):
                raw = a_pool.tile([P, TOKENS], BF16, tag="a_raw")
                nc.sync.dma_start(out=raw[:], in_=attention_blocks[b])
                a_raw[b] = raw

        def load_x_half(half):
            cols = slice(half * TOKENS // 2, (half + 1) * TOKENS // 2)
            nc.sync.dma_start(out=x_sb[:, :, cols], in_=x_tiles[:, :, cols])

        for g in range(M_PASSES):
            nc.sync.dma_start(
                out=v_raw[:, g].rearrange("q (u e) c -> q u (e c)", e=2), in_=v_passes[g]
            )
        load_attention(0)
        load_attention(1)
        nc.sync.dma_start(out=wo_raw[:], in_=wo_tiles)
        load_attention(2)
        load_x_half(0)
        load_attention(3)
        load_x_half(1)

        bo_rows = keep.tile([P, P], BF16)
        nc.vector.memset(bo_rows[:], 0.0)
        nc.scalar.dma_start(out=bo_rows[0:O_TILES, :], in_=bo_rows_dram)

        v_grouped = keep.tile([P, M_PASSES, CHANNELS, PACK], BF16, align_bytes=64)
        v_codes = keep.tile([P, M_PASSES, CHANNELS], U32, align_bytes=64)
        v_scales = keep.tile([P, M_PASSES, CHANNELS], U8, align_bytes=64)

        def group_v(copy, g, cols):
            copy(
                out=v_grouped[:, g, cols, :].rearrange("p (c i) t -> p c t i", i=4),
                in_=v_raw[:, g, :, cols].rearrange("p t (c i) -> p c t i", i=4),
            )

        for g in range(M_PASSES):
            group_v(nc.vector.tensor_copy, g, slice(0, V_COLUMNS_ON_VECTOR))
            group_v(nc.scalar.copy, g, slice(V_COLUMNS_ON_VECTOR, CHANNELS))
        for cols in (slice(0, CHANNELS // 2), slice(CHANNELS // 2, CHANNELS)):
            for g in range(M_PASSES):
                nc.vector.quantize_mx(
                    out=v_codes[:, g, cols].bitcast(FP8X4),
                    scales=v_scales[:, g, cols],
                    in_=v_grouped[:, g, cols, :].rearrange("p c t -> p (c t)"),
                )

        wo_grouped = keep.tile([P, O_TILES, P, PACK], BF16, align_bytes=64)
        wo_codes = keep.tile([P, CHANNELS], U32, align_bytes=64)
        wo_scales = keep.tile([P, CHANNELS], U8, align_bytes=64)
        bo_column = keep.tile([P, O_TILES], F32)

        def prepare_wo_and_bo():
            for o_tile in range(O_TILES):
                wo_psum = psum_t.tile([P, C_TILES, P], BF16, tag="transposed")
                for t in range(C_TILES):
                    nc.tensor.transpose(
                        wo_psum[:, t, :], wo_raw[:, o_tile, t * P : (t + 1) * P], identity_bf16[:]
                    )
                copy_out = nc.vector.tensor_copy if o_tile % 2 == 0 else nc.scalar.copy
                copy_out(out=wo_grouped[:, o_tile], in_=wo_psum[:].rearrange("p t o -> p o t"))
            bo_psum = psum_t.tile([P, P], BF16, tag="transposed")
            nc.tensor.transpose(bo_psum[:], bo_rows[:], identity_bf16[:])
            nc.vector.tensor_copy(out=bo_column[:], in_=bo_psum[:, 0:O_TILES])
            nc.vector.quantize_mx(
                out=wo_codes[:].bitcast(FP8X4),
                scales=wo_scales[:],
                in_=wo_grouped[:].rearrange("p k o t -> p (k o t)"),
            )

        a_codes = {}
        a_scales = {}
        h_codes = {}
        h_scales = {}

        def prepare(k):
            for b in range(k * CHUNK_BLOCKS, (k + 1) * CHUNK_BLOCKS):
                words = a_raw[b][:].bitcast(F32)
                transposed = psum_t.tile([P, M_PASSES * 2, P], F32, tag="transposed")
                for s in range(M_PASSES * 2):
                    nc.tensor.transpose(
                        transposed[:, s, :], words[:, s * P : (s + 1) * P], identity_f32[:]
                    )
                grouped = a_pool.tile(
                    [P, M_PASSES * P * PACK], BF16, tag="a_grouped", align_bytes=64
                )
                nc.scalar.copy(
                    out=grouped[:].bitcast(F32).rearrange("p (g n u) -> p g n u", g=M_PASSES, u=2),
                    in_=transposed[:].rearrange("p (g u) n -> p g n u", u=2),
                )
                codes = a_pool.tile([P, M_PASSES * P], U32, tag="a_codes", align_bytes=64)
                scales = a_pool.tile([P, M_PASSES * P], U8, tag="a_scales", align_bytes=64)
                nc.vector.quantize_mx(out=codes[:].bitcast(FP8X4), scales=scales[:], in_=grouped[:])
                a_codes[b] = codes
                a_scales[b] = scales

        def attend(k):
            grouped = h_pool.tile([P, CHUNK, PACK], BF16, tag="h_grouped", align_bytes=64)
            codes = h_pool.tile([P, CHUNK], U32, tag="h_codes", align_bytes=64)
            scales = h_pool.tile([P, CHUNK], U8, tag="h_scales", align_bytes=64)
            for j in range(CHUNK_BLOCKS):
                b = k * CHUNK_BLOCKS + j
                h_psum = psum_h.tile([P, C_TILES, P], F32, tag="h_psum")
                for t in range(C_TILES):
                    c_cols = slice(t * P, (t + 1) * P)
                    for g in range(M_PASSES):
                        g_cols = slice(g * P, (g + 1) * P)
                        nc.tensor.matmul_mx(
                            out=h_psum[:, t, :],
                            lhsT=v_codes[:, g, c_cols].bitcast(FP8X4),
                            lhsT_scale=v_scales[:, g, c_cols],
                            rhs=a_codes[b][:, g_cols].bitcast(FP8X4),
                            rhs_scale=a_scales[b][:, g_cols],
                            start=(g == 0),
                            stop=(g == M_PASSES - 1),
                        )
                n_cols = slice(j * P, (j + 1) * P)
                nc.scalar.copy(out=grouped[:, n_cols, :], in_=h_psum[:].rearrange("p t n -> p n t"))
                nc.vector.quantize_mx(
                    out=codes[:, n_cols].bitcast(FP8X4),
                    scales=scales[:, n_cols],
                    in_=grouped[:, n_cols, :].rearrange("p n t -> p (n t)"),
                )
            h_codes[k] = codes
            h_scales[k] = scales

        def project(k):
            n_cols = slice(k * CHUNK, (k + 1) * CHUNK)
            for bank_tiles in range(0, O_TILES, O_TILES_PER_BANK):
                p_psum = psum_p.tile([P, O_TILES_PER_BANK, CHUNK], F32, tag="p_psum")
                for i in range(O_TILES_PER_BANK):
                    o_tile = bank_tiles + i
                    o_cols = slice(o_tile * P, (o_tile + 1) * P)
                    nc.tensor.matmul_mx(
                        out=p_psum[:, i, :],
                        lhsT=wo_codes[:, o_cols].bitcast(FP8X4),
                        lhsT_scale=wo_scales[:, o_cols],
                        rhs=h_codes[k][:].bitcast(FP8X4),
                        rhs_scale=h_scales[k][:],
                        start=True,
                        stop=True,
                    )
                for i in range(O_TILES_PER_BANK):
                    o_tile = bank_tiles + i
                    y_sb = y_pool.tile([P, CHUNK], F32, tag="y_sb")
                    nc.vector.scalar_tensor_tensor(
                        out=y_sb[:],
                        in0=p_psum[:, i, :],
                        scalar=bo_column[:, o_tile : o_tile + 1],
                        in1=x_sb[:, o_tile, n_cols],
                        op0=ADD,
                        op1=ADD,
                    )
                    nc.sync.dma_start(out=y_tiles[:, o_tile, n_cols], in_=y_sb[:])

        prepare(0)
        prepare(1)
        attend(0)
        prepare_wo_and_bo()
        for k in range(CHUNKS):
            if k + 2 < CHUNKS:
                prepare(k + 2)
            project(k)
            if k + 1 < CHUNKS:
                attend(k + 1)
